import numpy as np
import ml_dtypes


def mxq(x, axis, fmt="e4m3"):
    dtype, down = {"e4m3": (ml_dtypes.float8_e4m3fn, 7), "e5m2": (ml_dtypes.float8_e5m2, 14)}[fmt]
    v = np.moveaxis(np.asarray(x, np.float32).astype(ml_dtypes.bfloat16).astype(np.float64), axis, -1)
    blocks = v.reshape(v.shape[:-1] + (-1, 32))
    amax = np.abs(blocks).max(-1, keepdims=True)
    byte = np.maximum(np.where(amax > 0, np.frexp(amax)[1] - 1 + 127, 0) - down, 1)
    scale = np.exp2(byte - 127.0)
    codes = (blocks / scale).astype(np.float32).astype(dtype).astype(np.float64)
    return np.moveaxis((codes * scale).reshape(v.shape), -1, axis)


WIDE = False


def mx_kscale(k):
    if not WIDE:
        return np.ones(k)
    levels = np.array([10, -10, 5, -5, 0])
    if k % 512:
        return np.exp2(np.random.permutation(np.resize(levels, k // 32))).repeat(32)
    a = np.empty((k // 512, 16))
    for p in range(k // 512):
        a[p, :8] = np.random.permutation(np.resize(levels, 8))
        for g in range(8):
            far = levels[np.abs(levels - a[p, g]) >= 10]
            a[p, g + 8] = far[np.random.randint(len(far))]
    return np.exp2(a.ravel()).repeat(32)


BF16 = ml_dtypes.bfloat16


def bf(x):
    return np.asarray(x, np.float32).astype(BF16)


def f64(x):
    return np.asarray(x).astype(np.float64)


B, Q, K, D = 2, 4096, 512, 1024
SIG = 2.0
PMASK = 0.1


def setup_inputs():
    s = mx_kscale(D)
    q = np.random.standard_normal((B, Q, D)) * s
    k = np.random.standard_normal((B, K, D)) * (SIG / np.sqrt(D)) / s
    k[:, :, 0] = np.where(np.random.random((B, K)) < PMASK, 0.0, k[:, :, 0])
    temperature = 1.0 + 0.1 * np.random.standard_normal(1)
    bias = -(np.log(K) + SIG ** 2 / 2.0) + 0.1 * np.random.standard_normal(1)
    return {"queries": bf(q), "keys": bf(k), "temperature": bf(temperature), "bias": bf(bias)}


def reference(queries, keys, temperature, bias):
    kf = f64(keys)
    logits = mxq(f64(queries), 2, "e4m3") @ mxq(kf, 2, "e4m3").transpose(0, 2, 1)
    key_mask = (kf[:, :, 0] == 0.0)[:, None, :]
    logits = np.where(key_mask, -np.inf, logits)
    m = logits.max(-1, keepdims=True)
    e = np.exp(logits - m)
    z = e.sum(-1, keepdims=True)
    approx_max_logit = (np.log(z) + m)[:, :, 0]
    confidence = 1.0 / (1.0 + np.exp(-((approx_max_logit + f64(bias)) * f64(temperature))))
    attn = e / z
    return attn, confidence

@@ -1,0 +1,271 @@
+from contextlib import ExitStack
+
+import concourse.mybir as mybir
+from concourse.masks import make_identity
+
+F32 = mybir.dt.float32
+BF16 = mybir.dt.bfloat16
+U32 = mybir.dt.uint32
+U8 = mybir.dt.uint8
+FP8X4 = mybir.dt.float8_e4m3fn_x4
+ALU = mybir.AluOpType
+ACT = mybir.ActivationFunctionType
+AX = mybir.AxisListType
+
+P = 128
+B, Q, K, D = 2, 4096, 512, 1024
+FLOPS = 2 * B * Q * K * D
+R = 4
+TILES_B = Q // P
+CHUNKS_B = TILES_B // R
+N_TILES = B * TILES_B
+N_PAIRS = N_TILES // 2
+BIG = 2.0 ** 120
+AHEAD = 8
+
+
+def tile_contentattention_t_kernel(tc, queries, keys, temperature, bias, out_0, out_1):
+    nc = tc.nc
+    with ExitStack() as ctx:
+        const = ctx.enter_context(tc.tile_pool(name="const", bufs=1))
+        qpool = ctx.enter_context(tc.tile_pool(name="qpool", bufs=10))
+        gpool = ctx.enter_context(tc.tile_pool(name="gpool", bufs=3))
+        cpool = ctx.enter_context(tc.tile_pool(name="cpool", bufs=4))
+        opool = ctx.enter_context(tc.tile_pool(name="opool", bufs=4))
+        ps_t = ctx.enter_context(tc.psum_pool(name="ps_t", bufs=4))
+        ps_l = ctx.enter_context(tc.psum_pool(name="ps_l", bufs=4))
+
+        one = const.tile([P, 1], F32, name="one")
+        junk = const.tile([P, 1], F32, name="junk")
+        nc.vector.memset(one[:], 1.0)
+        nc.scalar.activation(out=junk[:], in_=one[:], func=ACT.Exp)
+        ident_f = const.tile([P, P], F32, name="ident_f")
+        ident_b = const.tile([P, P], BF16, name="ident_b")
+        make_identity(nc, ident_f[:])
+        make_identity(nc, ident_b[:])
+
+        k_sb = const.tile([P, B * 4 * D], BF16, name="k_sb")
+        k32 = k_sb[:].bitcast(F32)
+        zsum = const.tile([P, N_TILES], F32, name="zsum")
+        negm = const.tile([P, N_TILES], F32, name="negm")
+        rz = const.tile([P, N_TILES], F32, name="rz")
+        t_bf = const.tile([P, 1], BF16, name="t_bf")
+        b_bf = const.tile([P, 1], BF16, name="b_bf")
+        t_f = const.tile([P, 1], F32, name="t_f")
+        t_b = const.tile([P, 1], F32, name="t_b")
+
+        q_tiles = {}
+
+        def load_keys(b):
+            for h in range(2):
+                nc.sync.dma_start(
+                    out=k_sb[:, (b * 4 + 2 * h) * D : (b * 4 + 2 * h + 2) * D].rearrange("p (t d) -> p t d", t=2),
+                    in_=keys[b][2 * h * P : (2 * h + 2) * P, :].rearrange("(t p) d -> p t d", p=P),
+                )
+
+        def load_chunk(c, pieces=1):
+            b, cc = divmod(c, CHUNKS_B)
+            q_sb = qpool.tile([P, R * D], BF16, name="q_sb")
+            w = R * D // pieces
+            for h in range(pieces):
+                nc.sync.dma_start(
+                    out=q_sb[:, h * w : (h + 1) * w],
+                    in_=queries[b].rearrange("(p r) d -> p (r d)", p=P)[:, cc * R * D + h * w : cc * R * D + (h + 1) * w],
+                )
+            q_tiles[c] = q_sb
+
+        kcodes, kscl, caps = {}, {}, {}
+
+        gks = {}
+
+        def keys_cap(b):
+            capv = const.tile([P, 4], BF16, name="capv%d" % b)
+            first = k_sb[:, b * 4 * D : (b + 1) * 4 * D].rearrange("p (t d) -> p t d", t=4)[:, :, 0:1]
+            nc.vector.tensor_scalar(out=capv[:].rearrange("p (t o) -> p t o", o=1), in0=first, scalar1=0.0, scalar2=-2.0 * BIG, op0=ALU.is_equal, op1=ALU.mult)
+            nc.vector.tensor_scalar_add(out=capv[:], in0=capv[:], scalar1=BIG)
+            cap_ps = ps_t.tile([P, K], F32, name="cap_ps", tag="xt")
+            for t in range(4):
+                nc.tensor.matmul(
+                    out=cap_ps[:, t * P : (t + 1) * P],
+                    lhsT=capv[:, t : t + 1].to_broadcast([P, P]),
+                    rhs=ident_b[:],
+                    start=True,
+                    stop=True,
+                )
+            cap = const.tile([P, K], F32, name="cap%d" % b)
+            nc.scalar.copy(out=cap[:], in_=cap_ps[:])
+            caps[b] = cap
+
+        def keys_transpose(b, t, on_vector):
+            if t == 0:
+                gk = const.tile([P, 2 * K * 4], BF16, name="gk%d" % b, align_bytes=64)
+                gks[b] = gk
+            gk32 = gks[b][:].bitcast(F32).rearrange("p (g j u) -> p g j u", g=2, u=2)
+            xt = ps_t.tile([P, 2, 2, P], F32, name="xt", tag="xt")
+            for w in range(4):
+                col = (b * 4 + t) * (D // 2) + (w // 2) * 2 * P + w % 2
+                nc.tensor.transpose(xt[:, w // 2, w % 2, :], k32[:, col : col + 2 * P - 1 : 2], ident_f[:])
+            dst = gk32[:, :, t * P : (t + 1) * P, :]
+            src = xt[:].rearrange("p g u r -> p g r u")
+            if on_vector:
+                nc.vector.tensor_copy(out=dst, in_=src)
+            else:
+                nc.scalar.copy(out=dst, in_=src)
+
+        def keys_quantise(b, g):
+            if g == 0:
+                kc = const.tile([P, 2 * K], U32, name="kc%d" % b, align_bytes=64)
+                ks = const.tile([P, 2 * K], U8, name="ks%d" % b, align_bytes=64)
+                kcodes[b], kscl[b] = kc, ks
+            nc.vector.quantize_mx(
+                out=kcodes[b][:, g * K : (g + 1) * K].bitcast(FP8X4),
+                scales=kscl[b][:, g * K : (g + 1) * K],
+                in_=gks[b][:, g * 4 * K : (g + 1) * 4 * K],
+            )
+
+        grps, codes, scls, lgs, outs = {}, {}, {}, {}, {}
+
+        def transpose_pair(i):
+            grp = gpool.tile([P, 2 * D], BF16, name="grp", align_bytes=64)
+            g32 = grp[:].bitcast(F32)
+            q32 = q_tiles[i // 2][:].bitcast(F32)
+            xts = []
+            for tl in range(2):
+                r = (i % 2) * 2 + tl
+                xt = ps_t.tile([P, 2, 2, P], F32, name="xt", tag="xt")
+                for w in range(4):
+                    col = r * (D // 2) + (w // 2) * 2 * P + w % 2
+                    nc.tensor.transpose(xt[:, w // 2, w % 2, :], q32[:, col : col + 2 * P - 1 : 2], ident_f[:])
+                xts.append(xt)
+            for tl in range(2):
+                nc.scalar.copy(
+                    out=g32[:, tl * 512 : (tl + 1) * 512].rearrange("p (g r u) -> p g r u", g=2, u=2),
+                    in_=xts[tl][:].rearrange("p g u r -> p g r u"),
+                )
+            grps[i] = grp
+
+        def quantise_pair(i):
+            cd = cpool.tile([P, 512], U32, name="cd", align_bytes=64)
+            sc = cpool.tile([P, 512], U8, name="sc", align_bytes=64)
+            nc.vector.quantize_mx(out=cd[:].bitcast(FP8X4), scales=sc[:], in_=grps[i][:])
+            codes[i], scls[i] = cd, sc
+
+        def logits_pair(i):
+            b = (2 * i) // TILES_B
+            for tl in range(2):
+                lg = ps_l.tile([P, K], F32, name="lg")
+                for g in range(2):
+                    s = (tl * 2 + g) * P
+                    nc.tensor.matmul_mx(
+                        out=lg[:],
+                        lhsT=codes[i][:, s : s + P].bitcast(FP8X4),
+                        lhsT_scale=scls[i][:, s : s + P],
+                        rhs=kcodes[b][:, g * K : (g + 1) * K].bitcast(FP8X4),
+                        rhs_scale=kscl[b][:, g * K : (g + 1) * K],
+                        start=(g == 0),
+                        stop=(g == 1),
+                    )
+                lgs[2 * i + tl] = lg
+
+        def out_slice(t):
+            return outs[t // R][:, (t % R) * K : (t % R + 1) * K]
+
+        def mask_max_pair(i):
+            b = (2 * i) // TILES_B
+            if i % 2 == 0:
+                ot = opool.tile([P, R * K], F32, name="ot")
+                outs[i // 2] = ot
+            for tl in range(2):
+                t = 2 * i + tl
+                nc.vector.tensor_tensor(out=out_slice(t), in0=lgs[t][:], in1=caps[b][:], op=ALU.min)
+            if i >= 1:
+                finish_pair(i - 1, False)
+            for tl in range(2):
+                t = 2 * i + tl
+                nc.vector.tensor_reduce(out=negm[:, t : t + 1], in_=out_slice(t), axis=AX.X, op=ALU.max, negate=True)
+
+        def exp_pair(i):
+            for tl in range(2):
+                t = 2 * i + tl
+                nc.scalar.activation(
+                    out=out_slice(t), in_=out_slice(t), func=ACT.Exp,
+                    bias=negm[:, t : t + 1], scale=1.0, accum_out=zsum[:, t : t + 1],
+                )
+
+        def store(t0, n):
+            b, r = divmod(t0, TILES_B)
+            nc.sync.dma_start(
+                out=out_0[b].rearrange("(p r) k -> p (r k)", p=P)[:, r * K : (r + n) * K],
+                in_=outs[t0 // R][:, (t0 % R) * K : (t0 % R + n) * K],
+            )
+
+        def finish_pair(i, last):
+            if not last:
+                nc.vector.reciprocal(out=rz[:, 2 * i : 2 * i + 2], in_=zsum[:, 2 * i : 2 * i + 2])
+            for tl in range(2):
+                t = 2 * i + tl
+                if last:
+                    nc.vector.reciprocal(out=rz[:, t : t + 1], in_=zsum[:, t : t + 1])
+                    nc.vector.tensor_scalar_mul(out=out_slice(t), in0=out_slice(t), scalar1=rz[:, t : t + 1])
+                    store(t, 1)
+                else:
+                    nc.gpsimd.tensor_scalar(
+                        out=out_slice(t), in0=out_slice(t), scalar1=rz[:, t : t + 1], scalar2=0.0,
+                        op0=ALU.mult, op1=ALU.add,
+                    )
+            if i == N_PAIRS - 2:
+                store(2 * i, 2)
+            elif i % 2 == 1 and not last:
+                store(2 * i - 2, 4)
+
+        ctx.enter_context(tc.manual_schedule())
+        load_keys(0)
+        load_chunk(0, 2)
+        load_chunk(1)
+        load_chunk(2)
+        load_keys(1)
+        nc.sync.dma_start(out=t_bf[:], in_=temperature.partition_broadcast(P))
+        nc.sync.dma_start(out=b_bf[:], in_=bias.partition_broadcast(P))
+        for c in range(3, AHEAD):
+            load_chunk(c)
+
+        for t in range(4):
+            keys_transpose(0, t, t % 2 == 1)
+        keys_cap(0)
+        transpose_pair(0)
+        keys_quantise(0, 0)
+        keys_quantise(0, 1)
+        transpose_pair(1)
+        quantise_pair(0)
+        logits_pair(0)
+        for i in range(N_PAIRS):
+            if i % 2 == 0 and i // 2 + AHEAD < B * CHUNKS_B:
+                load_chunk(i // 2 + AHEAD)
+            if i + 2 < N_PAIRS:
+                transpose_pair(i + 2)
+            if 4 <= i < 8:
+                keys_transpose(1, i - 4, False)
+            if i == 8:
+                keys_cap(1)
+            if i + 1 < N_PAIRS:
+                quantise_pair(i + 1)
+            if 9 <= i < 11:
+                keys_quantise(1, i - 9)
+            if i == 12:
+                nc.vector.tensor_copy(out=t_f[:], in_=t_bf[:])
+                nc.vector.tensor_tensor(out=t_b[:], in0=t_bf[:], in1=b_bf[:], op=ALU.mult)
+            mask_max_pair(i)
+            if i + 1 < N_PAIRS:
+                logits_pair(i + 1)
+            exp_pair(i)
+        finish_pair(N_PAIRS - 1, True)
+
+        lse = const.tile([P, N_TILES], F32, name="lse")
+        conf = const.tile([P, N_TILES], F32, name="conf")
+        nc.scalar.activation(out=lse[:], in_=zsum[:], func=ACT.Ln)
+        nc.vector.tensor_tensor(out=lse[:], in0=lse[:], in1=negm[:], op=ALU.subtract)
+        nc.scalar.activation(out=conf[:], in_=lse[:], func=ACT.Sigmoid, bias=t_b[:], scale=t_f[:])
+        nc.sync.dma_start(
+            out=out_1.rearrange("b (p r) -> p b r", p=P),
+            in_=conf[:].rearrange("p (b r) -> p b r", b=B),
+        )

@@ -31,7 +31,7 @@ def tile_contentattention_t_kernel(tc, queries, keys, temperature, bias, out_0, 
         qpool = ctx.enter_context(tc.tile_pool(name="qpool", bufs=10))
         gpool = ctx.enter_context(tc.tile_pool(name="gpool", bufs=3))
         cpool = ctx.enter_context(tc.tile_pool(name="cpool", bufs=4))
-        opool = ctx.enter_context(tc.tile_pool(name="opool", bufs=4))
+        opool = ctx.enter_context(tc.tile_pool(name="opool", bufs=5))
         ps_t = ctx.enter_context(tc.psum_pool(name="ps_t", bufs=4))
         ps_l = ctx.enter_context(tc.psum_pool(name="ps_l", bufs=4))
 
@@ -178,11 +178,15 @@ def tile_contentattention_t_kernel(tc, queries, keys, temperature, bias, out_0, 
             for tl in range(2):
                 t = 2 * i + tl
                 nc.vector.tensor_tensor(out=out_slice(t), in0=lgs[t][:], in1=caps[b][:], op=ALU.min)
-            if i >= 1:
+            if i == N_PAIRS - 1:
                 finish_pair(i - 1, False)
-            for tl in range(2):
-                t = 2 * i + tl
-                nc.vector.tensor_reduce(out=negm[:, t : t + 1], in_=out_slice(t), axis=AX.X, op=ALU.max, negate=True)
+            n = 1 if i == N_PAIRS - 1 else 2
+            for t in range(2 * i, 2 * i + 2, n):
+                nc.vector.tensor_reduce(
+                    out=negm[:, t : t + n],
+                    in_=outs[t // R][:, (t % R) * K : (t % R + n) * K].rearrange("p (t k) -> p t k", t=n),
+                    axis=AX.X, op=ALU.max, negate=True,
+                )
 
         def exp_pair(i):
             for tl in range(2):
@@ -254,6 +258,8 @@ def tile_contentattention_t_kernel(tc, queries, keys, temperature, bias, out_0, 
             if i == 12:
                 nc.vector.tensor_copy(out=t_f[:], in_=t_bf[:])
                 nc.vector.tensor_tensor(out=t_b[:], in0=t_bf[:], in1=b_bf[:], op=ALU.mult)
+            if i >= 2:
+                finish_pair(i - 2, False)
             mask_max_pair(i)
             if i + 1 < N_PAIRS:
                 logits_pair(i + 1)

@@ -180,13 +180,9 @@ def tile_contentattention_t_kernel(tc, queries, keys, temperature, bias, out_0, 
                 nc.vector.tensor_tensor(out=out_slice(t), in0=lgs[t][:], in1=caps[b][:], op=ALU.min)
             if i == N_PAIRS - 1:
                 finish_pair(i - 1, False)
-            n = 1 if i == N_PAIRS - 1 else 2
-            for t in range(2 * i, 2 * i + 2, n):
-                nc.vector.tensor_reduce(
-                    out=negm[:, t : t + n],
-                    in_=outs[t // R][:, (t % R) * K : (t % R + n) * K].rearrange("p (t k) -> p t k", t=n),
-                    axis=AX.X, op=ALU.max, negate=True,
-                )
+            for tl in range(2):
+                t = 2 * i + tl
+                nc.vector.tensor_reduce(out=negm[:, t : t + 1], in_=out_slice(t), axis=AX.X, op=ALU.max, negate=True)
 
         def exp_pair(i):
             for tl in range(2):

@@ -21,6 +21,9 @@ CHUNKS_B = TILES_B // R
 N_TILES = B * TILES_B
 N_PAIRS = N_TILES // 2
 BIG = 2.0 ** 120
+LAG = 2
+FIRST_TURNED = 8
+TURNED_EVERY = 5
 AHEAD = 8
 
 
@@ -29,8 +32,9 @@ def tile_contentattention_t_kernel(tc, queries, keys, temperature, bias, out_0, 
     with ExitStack() as ctx:
         const = ctx.enter_context(tc.tile_pool(name="const", bufs=1))
         qpool = ctx.enter_context(tc.tile_pool(name="qpool", bufs=10))
-        gpool = ctx.enter_context(tc.tile_pool(name="gpool", bufs=3))
+        gpool = ctx.enter_context(tc.tile_pool(name="gpool", bufs=5))
         cpool = ctx.enter_context(tc.tile_pool(name="cpool", bufs=4))
+        tpool = ctx.enter_context(tc.tile_pool(name="tpool", bufs=2))
         opool = ctx.enter_context(tc.tile_pool(name="opool", bufs=5))
         ps_t = ctx.enter_context(tc.psum_pool(name="ps_t", bufs=4))
         ps_l = ctx.enter_context(tc.psum_pool(name="ps_l", bufs=4))
@@ -56,25 +60,23 @@ def tile_contentattention_t_kernel(tc, queries, keys, temperature, bias, out_0, 
 
         q_tiles = {}
 
-        def load_keys(b):
-            for h in range(2):
-                nc.sync.dma_start(
-                    out=k_sb[:, (b * 4 + 2 * h) * D : (b * 4 + 2 * h + 2) * D].rearrange("p (t d) -> p t d", t=2),
-                    in_=keys[b][2 * h * P : (2 * h + 2) * P, :].rearrange("(t p) d -> p t d", p=P),
-                )
+        def load_keys(b, t, n):
+            nc.sync.dma_start(
+                out=k_sb[:, (b * 4 + t) * D : (b * 4 + t + n) * D].rearrange("p (t d) -> p t d", t=n),
+                in_=keys[b][t * P : (t + n) * P, :].rearrange("(t p) d -> p t d", p=P),
+            )
 
-        def load_chunk(c, pieces=1):
+        def load_rows(c, r, n):
             b, cc = divmod(c, CHUNKS_B)
-            q_sb = qpool.tile([P, R * D], BF16, name="q_sb")
-            w = R * D // pieces
-            for h in range(pieces):
-                nc.sync.dma_start(
-                    out=q_sb[:, h * w : (h + 1) * w],
-                    in_=queries[b].rearrange("(p r) d -> p (r d)", p=P)[:, cc * R * D + h * w : cc * R * D + (h + 1) * w],
-                )
-            q_tiles[c] = q_sb
+            if r == 0:
+                q_sb = qpool.tile([P, R * D], BF16, name="q_sb")
+                q_tiles[c] = q_sb
+            nc.sync.dma_start(
+                out=q_tiles[c][:, r * D : (r + n) * D],
+                in_=queries[b].rearrange("(p r) d -> p (r d)", p=P)[:, (cc * R + r) * D : (cc * R + r + n) * D],
+            )
 
-        kcodes, kscl, caps = {}, {}, {}
+        kcodes, kscl, caps, key_bias = {}, {}, {}, {}
 
         gks = {}
 
@@ -83,6 +85,12 @@ def tile_contentattention_t_kernel(tc, queries, keys, temperature, bias, out_0, 
             first = k_sb[:, b * 4 * D : (b + 1) * 4 * D].rearrange("p (t d) -> p t d", t=4)[:, :, 0:1]
             nc.vector.tensor_scalar(out=capv[:].rearrange("p (t o) -> p t o", o=1), in0=first, scalar1=0.0, scalar2=-2.0 * BIG, op0=ALU.is_equal, op1=ALU.mult)
             nc.vector.tensor_scalar_add(out=capv[:], in0=capv[:], scalar1=BIG)
+            bias_b = const.tile([P, 4], F32, name="key_bias%d" % b)
+            nc.vector.tensor_scalar(out=bias_b[:].rearrange("p (t o) -> p t o", o=1), in0=first, scalar1=0.0, scalar2=-BIG, op0=ALU.is_equal, op1=ALU.mult)
+            key_bias[b] = bias_b
+            return capv
+
+        def keys_cap_row(b, capv):
             cap_ps = ps_t.tile([P, K], F32, name="cap_ps", tag="xt")
             for t in range(4):
                 nc.tensor.matmul(
@@ -97,65 +105,119 @@ def tile_contentattention_t_kernel(tc, queries, keys, temperature, bias, out_0, 
             caps[b] = cap
 
         def keys_transpose(b, t, on_vector):
-            if t == 0:
-                gk = const.tile([P, 2 * K * 4], BF16, name="gk%d" % b, align_bytes=64)
-                gks[b] = gk
-            gk32 = gks[b][:].bitcast(F32).rearrange("p (g j u) -> p g j u", g=2, u=2)
+            if t % 2 == 0:
+                gk = const.tile([P, 2 * K * 2], BF16, name="gk%d_%d" % (b, t), align_bytes=64)
+                gks[b, t // 2] = gk
+            gk32 = gks[b, t // 2][:].bitcast(F32).rearrange("p (g j u) -> p g j u", g=2, u=2)
             xt = ps_t.tile([P, 2, 2, P], F32, name="xt", tag="xt")
             for w in range(4):
                 col = (b * 4 + t) * (D // 2) + (w // 2) * 2 * P + w % 2
                 nc.tensor.transpose(xt[:, w // 2, w % 2, :], k32[:, col : col + 2 * P - 1 : 2], ident_f[:])
-            dst = gk32[:, :, t * P : (t + 1) * P, :]
+            dst = gk32[:, :, (t % 2) * P : (t % 2 + 1) * P, :]
             src = xt[:].rearrange("p g u r -> p g r u")
             if on_vector:
                 nc.vector.tensor_copy(out=dst, in_=src)
             else:
                 nc.scalar.copy(out=dst, in_=src)
 
-        def keys_quantise(b, g):
-            if g == 0:
+        def keys_quantise(b, h, g):
+            if g == 0 and h == 0:
                 kc = const.tile([P, 2 * K], U32, name="kc%d" % b, align_bytes=64)
                 ks = const.tile([P, 2 * K], U8, name="ks%d" % b, align_bytes=64)
                 kcodes[b], kscl[b] = kc, ks
             nc.vector.quantize_mx(
-                out=kcodes[b][:, g * K : (g + 1) * K].bitcast(FP8X4),
-                scales=kscl[b][:, g * K : (g + 1) * K],
-                in_=gks[b][:, g * 4 * K : (g + 1) * 4 * K],
+                out=kcodes[b][:, g * K + h * 2 * P : g * K + (h + 1) * 2 * P].bitcast(FP8X4),
+                scales=kscl[b][:, g * K + h * 2 * P : g * K + (h + 1) * 2 * P],
+                in_=gks[b, h][:, g * 8 * P : (g + 1) * 8 * P],
             )
 
-        grps, codes, scls, lgs, outs = {}, {}, {}, {}, {}
+        xts, grps, codes, scls, lgs, lts, outs = {}, {}, {}, {}, {}, {}, {}
+
+        def transpose_tile(t):
+            i, tl = divmod(t, 2)
+            if tl == 0:
+                grp = gpool.tile([P, 2 * D], BF16, name="grp", align_bytes=64)
+                grps[i] = grp
+            q32 = q_tiles[t // R][:].bitcast(F32)
+            xt = ps_t.tile([P, 2, 2, P], F32, name="xt", tag="xt")
+            for w in range(4):
+                col = (t % R) * (D // 2) + (w // 2) * 2 * P + w % 2
+                nc.tensor.transpose(xt[:, w // 2, w % 2, :], q32[:, col : col + 2 * P - 1 : 2], ident_f[:])
+            xts[t] = xt
+
+        def copy_tile(t, on_vector):
+            i, tl = divmod(t, 2)
+            g32 = grps[i][:].bitcast(F32)
+            if i == 0:
+                dst = g32[:, tl * 512 : (tl + 1) * 512].rearrange("p (g r u) -> p g r u", g=2, u=2)
+            else:
+                dst = g32.rearrange("p (g t r u) -> p g t r u", g=2, t=2, u=2)[:, :, tl, :, :]
+            src = xts[t][:].rearrange("p g u r -> p g r u")
+            if on_vector:
+                nc.vector.tensor_copy(out=dst, in_=src)
+            else:
+                nc.scalar.copy(out=dst, in_=src)
 
         def transpose_pair(i):
-            grp = gpool.tile([P, 2 * D], BF16, name="grp", align_bytes=64)
-            g32 = grp[:].bitcast(F32)
-            q32 = q_tiles[i // 2][:].bitcast(F32)
-            xts = []
-            for tl in range(2):
-                r = (i % 2) * 2 + tl
-                xt = ps_t.tile([P, 2, 2, P], F32, name="xt", tag="xt")
-                for w in range(4):
-                    col = r * (D // 2) + (w // 2) * 2 * P + w % 2
-                    nc.tensor.transpose(xt[:, w // 2, w % 2, :], q32[:, col : col + 2 * P - 1 : 2], ident_f[:])
-                xts.append(xt)
-            for tl in range(2):
-                nc.scalar.copy(
-                    out=g32[:, tl * 512 : (tl + 1) * 512].rearrange("p (g r u) -> p g r u", g=2, u=2),
-                    in_=xts[tl][:].rearrange("p g u r -> p g r u"),
-                )
-            grps[i] = grp
+            for t in (2 * i, 2 * i + 1):
+                transpose_tile(t)
 
-        def quantise_pair(i):
-            cd = cpool.tile([P, 512], U32, name="cd", align_bytes=64)
-            sc = cpool.tile([P, 512], U8, name="sc", align_bytes=64)
-            nc.vector.quantize_mx(out=cd[:].bitcast(FP8X4), scales=sc[:], in_=grps[i][:])
-            codes[i], scls[i] = cd, sc
+        def copy_pair(i):
+            for t in (2 * i, 2 * i + 1):
+                copy_tile(t, False)
+
+        def quantise(i, tl, n):
+            if tl == 0:
+                cd = cpool.tile([P, 512], U32, name="cd", align_bytes=64)
+                sc = cpool.tile([P, 512], U8, name="sc", align_bytes=64)
+                codes[i], scls[i] = cd, sc
+            nc.vector.quantize_mx(
+                out=codes[i][:, tl * 256 : (tl + n) * 256].bitcast(FP8X4),
+                scales=scls[i][:, tl * 256 : (tl + n) * 256],
+                in_=grps[i][:, tl * D : (tl + n) * D],
+            )
+
+        def turned(i):
+            return i >= FIRST_TURNED and (i - FIRST_TURNED) % TURNED_EVERY == 0 and i + 2 < N_PAIRS - 1
+
+        def logits_turned(i):
+            b = (2 * i) // TILES_B
+            lt = tpool.tile([P, 4, 2 * P], F32, name="lt")
+            for h in range(2):
+                lg = ps_l.tile([P, K], F32, name="lg")
+                for e in range(2):
+                    kt = 2 * h + e
+                    for g in range(2):
+                        nc.tensor.matmul_mx(
+                            out=lg[:, e * 2 * P : (e + 1) * 2 * P],
+                            lhsT=kcodes[b][:, g * K + kt * P : g * K + (kt + 1) * P].bitcast(FP8X4),
+                            lhsT_scale=kscl[b][:, g * K + kt * P : g * K + (kt + 1) * P],
+                            rhs=codes[i][:, g * 2 * P : (g + 1) * 2 * P].bitcast(FP8X4),
+                            rhs_scale=scls[i][:, g * 2 * P : (g + 1) * 2 * P],
+                            start=(g == 0),
+                            stop=(g == 1),
+                        )
+                for e in range(2):
+                    kt = 2 * h + e
+                    nc.scalar.activation(
+                        out=lt[:, kt, :], in_=lg[:, e * 2 * P : (e + 1) * 2 * P], func=ACT.Identity,
+                        bias=key_bias[b][:, kt : kt + 1], scale=1.0,
+                    )
+            lts[i] = lt
+
+        def turn_back(i):
+            for tl in range(2):
+                lg = ps_l.tile([P, K], F32, name="lg")
+                for kt in range(4):
+                    nc.tensor.transpose(lg[:, kt * P : (kt + 1) * P], lts[i][:, kt, tl * P : (tl + 1) * P], ident_f[:])
+                lgs[2 * i + tl] = lg
 
         def logits_pair(i):
             b = (2 * i) // TILES_B
             for tl in range(2):
                 lg = ps_l.tile([P, K], F32, name="lg")
                 for g in range(2):
-                    s = (tl * 2 + g) * P
+                    s = (tl * 2 + g if i == 0 else g * 2 + tl) * P
                     nc.tensor.matmul_mx(
                         out=lg[:],
                         lhsT=codes[i][:, s : s + P].bitcast(FP8X4),
@@ -170,25 +232,27 @@ def tile_contentattention_t_kernel(tc, queries, keys, temperature, bias, out_0, 
         def out_slice(t):
             return outs[t // R][:, (t % R) * K : (t % R + 1) * K]
 
-        def mask_max_pair(i):
+        def mask_pair(i):
             b = (2 * i) // TILES_B
             if i % 2 == 0:
                 ot = opool.tile([P, R * K], F32, name="ot")
                 outs[i // 2] = ot
             for tl in range(2):
                 t = 2 * i + tl
-                nc.vector.tensor_tensor(out=out_slice(t), in0=lgs[t][:], in1=caps[b][:], op=ALU.min)
-            if i == N_PAIRS - 1:
-                finish_pair(i - 1, False)
+                if not turned(i):
+                    nc.vector.tensor_tensor(out=out_slice(t), in0=lgs[t][:], in1=caps[b][:], op=ALU.min)
+
+        def max_pair(i):
             for tl in range(2):
                 t = 2 * i + tl
-                nc.vector.tensor_reduce(out=negm[:, t : t + 1], in_=out_slice(t), axis=AX.X, op=ALU.max, negate=True)
+                src = lgs[t][:] if turned(i) else out_slice(t)
+                nc.vector.tensor_reduce(out=negm[:, t : t + 1], in_=src, axis=AX.X, op=ALU.max, negate=True)
 
         def exp_pair(i):
             for tl in range(2):
                 t = 2 * i + tl
                 nc.scalar.activation(
-                    out=out_slice(t), in_=out_slice(t), func=ACT.Exp,
+                    out=out_slice(t), in_=lgs[t][:] if turned(i) else out_slice(t), func=ACT.Exp,
                     bias=negm[:, t : t + 1], scale=1.0, accum_out=zsum[:, t : t + 1],
                 )
 
@@ -199,15 +263,12 @@ def tile_contentattention_t_kernel(tc, queries, keys, temperature, bias, out_0, 
                 in_=outs[t0 // R][:, (t0 % R) * K : (t0 % R + n) * K],
             )
 
-        def finish_pair(i, last):
-            if not last:
-                nc.vector.reciprocal(out=rz[:, 2 * i : 2 * i + 2], in_=zsum[:, 2 * i : 2 * i + 2])
+        def finish_pair(i, n_vector):
+            nc.vector.reciprocal(out=rz[:, 2 * i : 2 * i + 2], in_=zsum[:, 2 * i : 2 * i + 2])
             for tl in range(2):
                 t = 2 * i + tl
-                if last:
-                    nc.vector.reciprocal(out=rz[:, t : t + 1], in_=zsum[:, t : t + 1])
+                if tl >= 2 - n_vector:
                     nc.vector.tensor_scalar_mul(out=out_slice(t), in0=out_slice(t), scalar1=rz[:, t : t + 1])
-                    store(t, 1)
                 else:
                     nc.gpsimd.tensor_scalar(
                         out=out_slice(t), in0=out_slice(t), scalar1=rz[:, t : t + 1], scalar2=0.0,
@@ -215,52 +276,89 @@ def tile_contentattention_t_kernel(tc, queries, keys, temperature, bias, out_0, 
                     )
             if i == N_PAIRS - 2:
                 store(2 * i, 2)
-            elif i % 2 == 1 and not last:
+            elif i % 2 == 1:
                 store(2 * i - 2, 4)
 
+        def finish_last():
+            for t in range(N_TILES - 2, N_TILES):
+                nc.vector.reciprocal(out=rz[:, t : t + 1], in_=zsum[:, t : t + 1])
+                nc.vector.tensor_scalar_mul(out=out_slice(t), in0=out_slice(t), scalar1=rz[:, t : t + 1])
+                store(t, 1)
+
         ctx.enter_context(tc.manual_schedule())
-        load_keys(0)
-        load_chunk(0, 2)
-        load_chunk(1)
-        load_chunk(2)
-        load_keys(1)
+        load_rows(0, 0, 1)
+        for t in range(4):
+            load_keys(0, t, 1)
+        load_rows(0, 1, 1)
+        load_rows(0, 2, 2)
+        load_rows(1, 0, R)
+        load_rows(2, 0, R)
+        load_keys(1, 0, 4)
         nc.sync.dma_start(out=t_bf[:], in_=temperature.partition_broadcast(P))
         nc.sync.dma_start(out=b_bf[:], in_=bias.partition_broadcast(P))
         for c in range(3, AHEAD):
-            load_chunk(c)
+            load_rows(c, 0, R)
 
-        for t in range(4):
-            keys_transpose(0, t, t % 2 == 1)
-        keys_cap(0)
-        transpose_pair(0)
-        keys_quantise(0, 0)
-        keys_quantise(0, 1)
+        transpose_tile(0)
+        copy_tile(0, False)
+        keys_transpose(0, 0, True)
+        keys_transpose(0, 1, False)
+        quantise(0, 0, 1)
+        keys_transpose(0, 2, True)
+        keys_transpose(0, 3, False)
+        capv = keys_cap(0)
+        for h in range(2):
+            for g in range(2):
+                keys_quantise(0, h, g)
+        transpose_tile(1)
+        copy_tile(1, False)
+        quantise(0, 1, 1)
+        keys_cap_row(0, capv)
         transpose_pair(1)
-        quantise_pair(0)
+        copy_pair(1)
         logits_pair(0)
+        transpose_pair(2)
+        copy_pair(2)
         for i in range(N_PAIRS):
             if i % 2 == 0 and i // 2 + AHEAD < B * CHUNKS_B:
-                load_chunk(i // 2 + AHEAD)
-            if i + 2 < N_PAIRS:
-                transpose_pair(i + 2)
+                load_rows(i // 2 + AHEAD, 0, R)
+            if turned(i):
+                turn_back(i)
+            if i + 3 < N_PAIRS:
+                transpose_pair(i + 3)
+                if not turned(i + 1):
+                    copy_pair(i + 3)
             if 4 <= i < 8:
                 keys_transpose(1, i - 4, False)
+            if i == 6:
+                capv = keys_cap(1)
             if i == 8:
-                keys_cap(1)
-            if i + 1 < N_PAIRS:
-                quantise_pair(i + 1)
+                keys_cap_row(1, capv)
+            if 1 <= i < N_PAIRS - 1:
+                quantise(i + 1, 0, 2)
             if 9 <= i < 11:
-                keys_quantise(1, i - 9)
+                for g in range(2):
+                    keys_quantise(1, i - 9, g)
             if i == 12:
                 nc.vector.tensor_copy(out=t_f[:], in_=t_bf[:])
                 nc.vector.tensor_tensor(out=t_b[:], in0=t_bf[:], in1=b_bf[:], op=ALU.mult)
-            if i >= 2:
-                finish_pair(i - 2, False)
-            mask_max_pair(i)
+            if i >= LAG:
+                finish_pair(i - LAG, 1 if turned(i) else 0)
+            mask_pair(i)
+            if i == 0:
+                quantise(1, 0, 2)
+            if i == N_PAIRS - 1:
+                for j in range(i - LAG + 1, i):
+                    finish_pair(j, 0)
+            max_pair(i)
             if i + 1 < N_PAIRS:
-                logits_pair(i + 1)
+                if turned(i + 1):
+                    logits_turned(i + 1)
+                    copy_pair(i + 3)
+                else:
+                    logits_pair(i + 1)
             exp_pair(i)
-        finish_pair(N_PAIRS - 1, True)
+        finish_last()
 
         lse = const.tile([P, N_TILES], F32, name="lse")
         conf = const.tile([P, N_TILES], F32, name="conf")

@@ -22,8 +22,8 @@ N_TILES = B * TILES_B
 N_PAIRS = N_TILES // 2
 BIG = 2.0 ** 120
 LAG = 2
-FIRST_TURNED = 8
-TURNED_EVERY = 5
+FIRST_TURNED = 9
+TURNED_EVERY = 7
 AHEAD = 8
 
 
@@ -178,7 +178,7 @@ def tile_contentattention_t_kernel(tc, queries, keys, temperature, bias, out_0, 
             )
 
         def turned(i):
-            return i >= FIRST_TURNED and (i - FIRST_TURNED) % TURNED_EVERY == 0 and i + 2 < N_PAIRS - 1
+            return i >= FIRST_TURNED and (i - FIRST_TURNED) % TURNED_EVERY == 0
 
         def logits_turned(i):
             b = (2 * i) // TILES_B
@@ -354,7 +354,8 @@ def tile_contentattention_t_kernel(tc, queries, keys, temperature, bias, out_0, 
             if i + 1 < N_PAIRS:
                 if turned(i + 1):
                     logits_turned(i + 1)
-                    copy_pair(i + 3)
+                    if i + 3 < N_PAIRS:
+                        copy_pair(i + 3)
                 else:
                     logits_pair(i + 1)
             exp_pair(i)

@@ -22,8 +22,8 @@ N_TILES = B * TILES_B
 N_PAIRS = N_TILES // 2
 BIG = 2.0 ** 120
 LAG = 2
-FIRST_TURNED = 9
-TURNED_EVERY = 7
+FIRST_TURNED = 10
+TURNED_EVERY = 5
 AHEAD = 8
 
 
@@ -133,6 +133,9 @@ def tile_contentattention_t_kernel(tc, queries, keys, temperature, bias, out_0, 
 
         xts, grps, codes, scls, lgs, lts, outs = {}, {}, {}, {}, {}, {}, {}
 
+        def turned(i):
+            return i >= FIRST_TURNED and (i - FIRST_TURNED) % TURNED_EVERY == 0
+
         def transpose_tile(t):
             i, tl = divmod(t, 2)
             if tl == 0:
@@ -148,7 +151,7 @@ def tile_contentattention_t_kernel(tc, queries, keys, temperature, bias, out_0, 
         def copy_tile(t, on_vector):
             i, tl = divmod(t, 2)
             g32 = grps[i][:].bitcast(F32)
-            if i == 0:
+            if not turned(i):
                 dst = g32[:, tl * 512 : (tl + 1) * 512].rearrange("p (g r u) -> p g r u", g=2, u=2)
             else:
                 dst = g32.rearrange("p (g t r u) -> p g t r u", g=2, t=2, u=2)[:, :, tl, :, :]
@@ -176,9 +179,6 @@ def tile_contentattention_t_kernel(tc, queries, keys, temperature, bias, out_0, 
                 scales=scls[i][:, tl * 256 : (tl + n) * 256],
                 in_=grps[i][:, tl * D : (tl + n) * D],
             )
-
-        def turned(i):
-            return i >= FIRST_TURNED and (i - FIRST_TURNED) % TURNED_EVERY == 0
 
         def logits_turned(i):
             b = (2 * i) // TILES_B
@@ -217,7 +217,7 @@ def tile_contentattention_t_kernel(tc, queries, keys, temperature, bias, out_0, 
             for tl in range(2):
                 lg = ps_l.tile([P, K], F32, name="lg")
                 for g in range(2):
-                    s = (tl * 2 + g if i == 0 else g * 2 + tl) * P
+                    s = (tl * 2 + g) * P
                     nc.tensor.matmul_mx(
                         out=lg[:],
                         lhsT=codes[i][:, s : s + P].bitcast(FP8X4),
@@ -290,8 +290,10 @@ def tile_contentattention_t_kernel(tc, queries, keys, temperature, bias, out_0, 
         for t in range(4):
             load_keys(0, t, 1)
         load_rows(0, 1, 1)
-        load_rows(0, 2, 2)
-        load_rows(1, 0, R)
+        load_rows(0, 2, 1)
+        load_rows(0, 3, 1)
+        load_rows(1, 0, 2)
+        load_rows(1, 2, 2)
         load_rows(2, 0, R)
         load_keys(1, 0, 4)
         nc.sync.dma_start(out=t_bf[:], in_=temperature.partition_broadcast(P))

@@ -22,8 +22,12 @@ N_TILES = B * TILES_B
 N_PAIRS = N_TILES // 2
 BIG = 2.0 ** 120
 LAG = 2
-FIRST_TURNED = 10
-TURNED_EVERY = 5
+LN_AT = N_PAIRS - 4
+N_EARLY = 2 * (LN_AT + 1)
+N_LATE = N_TILES - N_EARLY
+FIRST_TURNED = 9
+TURNED_EVERY = 4
+TURNED_BEFORE = LN_AT - 1
 AHEAD = 8
 
 
@@ -55,8 +59,13 @@ def tile_contentattention_t_kernel(tc, queries, keys, temperature, bias, out_0, 
         rz = const.tile([P, N_TILES], F32, name="rz")
         t_bf = const.tile([P, 1], BF16, name="t_bf")
         b_bf = const.tile([P, 1], BF16, name="b_bf")
-        t_f = const.tile([P, 1], F32, name="t_f")
+        t_n = const.tile([P, 1], F32, name="t_n")
         t_b = const.tile([P, 1], F32, name="t_b")
+        lse = const.tile([P, N_EARLY], F32, name="lse")
+        early = const.tile([P, N_EARLY], F32, name="early")
+        late = const.tile([P, N_LATE], F32, name="late")
+        conf = const.tile([P, N_TILES], F32, name="conf")
+        den = const.tile([P, N_EARLY], F32, name="den")
 
         q_tiles = {}
 
@@ -83,8 +92,7 @@ def tile_contentattention_t_kernel(tc, queries, keys, temperature, bias, out_0, 
         def keys_cap(b):
             capv = const.tile([P, 4], BF16, name="capv%d" % b)
             first = k_sb[:, b * 4 * D : (b + 1) * 4 * D].rearrange("p (t d) -> p t d", t=4)[:, :, 0:1]
-            nc.vector.tensor_scalar(out=capv[:].rearrange("p (t o) -> p t o", o=1), in0=first, scalar1=0.0, scalar2=-2.0 * BIG, op0=ALU.is_equal, op1=ALU.mult)
-            nc.vector.tensor_scalar_add(out=capv[:], in0=capv[:], scalar1=BIG)
+            nc.vector.tensor_scalar(out=capv[:].rearrange("p (t o) -> p t o", o=1), in0=first, scalar1=0.0, scalar2=-0.5, op0=ALU.not_equal, op1=ALU.add)
             bias_b = const.tile([P, 4], F32, name="key_bias%d" % b)
             nc.vector.tensor_scalar(out=bias_b[:].rearrange("p (t o) -> p t o", o=1), in0=first, scalar1=0.0, scalar2=-BIG, op0=ALU.is_equal, op1=ALU.mult)
             key_bias[b] = bias_b
@@ -101,7 +109,7 @@ def tile_contentattention_t_kernel(tc, queries, keys, temperature, bias, out_0, 
                     stop=True,
                 )
             cap = const.tile([P, K], F32, name="cap%d" % b)
-            nc.scalar.copy(out=cap[:], in_=cap_ps[:])
+            nc.scalar.mul(out=cap[:], in_=cap_ps[:], mul=2.0 * BIG)
             caps[b] = cap
 
         def keys_transpose(b, t, on_vector):
@@ -134,7 +142,7 @@ def tile_contentattention_t_kernel(tc, queries, keys, temperature, bias, out_0, 
         xts, grps, codes, scls, lgs, lts, outs = {}, {}, {}, {}, {}, {}, {}
 
         def turned(i):
-            return i >= FIRST_TURNED and (i - FIRST_TURNED) % TURNED_EVERY == 0
+            return FIRST_TURNED <= i < TURNED_BEFORE and (i - FIRST_TURNED) % TURNED_EVERY == 0
 
         def transpose_tile(t):
             i, tl = divmod(t, 2)
@@ -242,15 +250,15 @@ def tile_contentattention_t_kernel(tc, queries, keys, temperature, bias, out_0, 
                 if not turned(i):
                     nc.vector.tensor_tensor(out=out_slice(t), in0=lgs[t][:], in1=caps[b][:], op=ALU.min)
 
-        def max_pair(i):
-            for tl in range(2):
-                t = 2 * i + tl
-                src = lgs[t][:] if turned(i) else out_slice(t)
-                nc.vector.tensor_reduce(out=negm[:, t : t + 1], in_=src, axis=AX.X, op=ALU.max, negate=True)
+        def row_max(t):
+            src = lgs[t][:] if turned(t // 2) else out_slice(t)
+            nc.vector.tensor_reduce(out=negm[:, t : t + 1], in_=src, axis=AX.X, op=ALU.max, negate=True)
 
         def exp_pair(i):
             for tl in range(2):
                 t = 2 * i + tl
+                if t == N_TILES - 1:
+                    exp_m_late()
                 nc.scalar.activation(
                     out=out_slice(t), in_=lgs[t][:] if turned(i) else out_slice(t), func=ACT.Exp,
                     bias=negm[:, t : t + 1], scale=1.0, accum_out=zsum[:, t : t + 1],
@@ -263,27 +271,54 @@ def tile_contentattention_t_kernel(tc, queries, keys, temperature, bias, out_0, 
                 in_=outs[t0 // R][:, (t0 % R) * K : (t0 % R + n) * K],
             )
 
-        def finish_pair(i, n_vector):
-            nc.vector.reciprocal(out=rz[:, 2 * i : 2 * i + 2], in_=zsum[:, 2 * i : 2 * i + 2])
-            for tl in range(2):
-                t = 2 * i + tl
-                if tl >= 2 - n_vector:
-                    nc.vector.tensor_scalar_mul(out=out_slice(t), in0=out_slice(t), scalar1=rz[:, t : t + 1])
-                else:
-                    nc.gpsimd.tensor_scalar(
-                        out=out_slice(t), in0=out_slice(t), scalar1=rz[:, t : t + 1], scalar2=0.0,
-                        op0=ALU.mult, op1=ALU.add,
-                    )
-            if i == N_PAIRS - 2:
+        def invert(t, n):
+            nc.vector.reciprocal(out=rz[:, t : t + n], in_=zsum[:, t : t + n])
+
+        def scale_tile(t, on_vector):
+            o = out_slice(t)
+            if on_vector:
+                nc.vector.tensor_scalar_mul(out=o, in0=o, scalar1=rz[:, t : t + 1])
+            else:
+                nc.gpsimd.tensor_scalar(out=o, in0=o, scalar1=rz[:, t : t + 1], scalar2=0.0, op0=ALU.mult, op1=ALU.add)
+
+        def store_pair(i):
+            if i >= N_PAIRS - 4:
                 store(2 * i, 2)
             elif i % 2 == 1:
                 store(2 * i - 2, 4)
 
+        def log_early():
+            nc.scalar.activation(out=lse[:], in_=zsum[:, 0:N_EARLY], func=ACT.Ln)
+
+        def lse_early():
+            nc.gpsimd.tensor_tensor(out=lse[:], in0=lse[:], in1=negm[:, 0:N_EARLY], op=ALU.subtract)
+
+        def conf_early():
+            nc.scalar.activation(out=early[:], in_=lse[:], func=ACT.Exp, bias=t_b[:], scale=t_n[:])
+            nc.gpsimd.tensor_scalar(out=den[:], in0=early[:], scalar1=1.0, scalar2=1.0, op0=ALU.mult, op1=ALU.add)
+
+        def exp_m_late():
+            nc.scalar.activation(out=late[:], in_=negm[:, N_EARLY:], func=ACT.Exp, bias=b_bf[:], scale=-1.0)
+
+        last = const.tile([P, N_LATE], F32, name="last")
+        last_p = const.tile([P, N_LATE], F32, name="last_p")
+
         def finish_last():
-            for t in range(N_TILES - 2, N_TILES):
-                nc.vector.reciprocal(out=rz[:, t : t + 1], in_=zsum[:, t : t + 1])
-                nc.vector.tensor_scalar_mul(out=out_slice(t), in0=out_slice(t), scalar1=rz[:, t : t + 1])
+            t0 = N_TILES - 4
+            invert(t0, 2)
+            invert(t0 + 2, 1)
+            for t in (t0, t0 + 1):
+                scale_tile(t, True)
+            store(t0, 2)
+            nc.vector.tensor_tensor(out=last[:], in0=zsum[:, N_EARLY:], in1=late[:], op=ALU.mult)
+            nc.gpsimd.tensor_tensor(out=last_p[:], in0=last[:], in1=t_n[:].to_broadcast([P, N_LATE]), op=ALU.pow)
+            invert(t0 + 3, 1)
+            for t in (t0 + 2, t0 + 3):
+                nc.scalar.activation(out=out_slice(t), in_=out_slice(t), func=ACT.Copy, scale=rz[:, t : t + 1])
                 store(t, 1)
+            nc.vector.reciprocal(out=conf[:, 0:N_EARLY], in_=den[:])
+            nc.vector.tensor_scalar_add(out=last[:], in0=last_p[:], scalar1=1.0)
+            nc.vector.reciprocal(out=conf[:, N_EARLY:], in_=last[:])
 
         ctx.enter_context(tc.manual_schedule())
         load_rows(0, 0, 1)
@@ -342,17 +377,23 @@ def tile_contentattention_t_kernel(tc, queries, keys, temperature, bias, out_0, 
                 for g in range(2):
                     keys_quantise(1, i - 9, g)
             if i == 12:
-                nc.vector.tensor_copy(out=t_f[:], in_=t_bf[:])
-                nc.vector.tensor_tensor(out=t_b[:], in0=t_bf[:], in1=b_bf[:], op=ALU.mult)
+                nc.gpsimd.tensor_scalar(out=t_n[:], in0=t_bf[:], scalar1=-1.0, scalar2=0.0, op0=ALU.mult, op1=ALU.add)
+                nc.gpsimd.tensor_tensor(out=t_b[:], in0=t_n[:], in1=b_bf[:], op=ALU.mult)
             if i >= LAG:
-                finish_pair(i - LAG, 1 if turned(i) else 0)
+                j = i - LAG
+                invert(2 * j, 2)
+                scale_tile(2 * j, False)
+                if not turned(i):
+                    scale_tile(2 * j + 1, False)
+                    store_pair(j)
             mask_pair(i)
             if i == 0:
                 quantise(1, 0, 2)
-            if i == N_PAIRS - 1:
-                for j in range(i - LAG + 1, i):
-                    finish_pair(j, 0)
-            max_pair(i)
+            row_max(2 * i)
+            if turned(i):
+                scale_tile(2 * j + 1, True)
+                store_pair(j)
+            row_max(2 * i + 1)
             if i + 1 < N_PAIRS:
                 if turned(i + 1):
                     logits_turned(i + 1)
@@ -360,14 +401,14 @@ def tile_contentattention_t_kernel(tc, queries, keys, temperature, bias, out_0, 
                         copy_pair(i + 3)
                 else:
                     logits_pair(i + 1)
+            if i == N_PAIRS - 1:
+                conf_early()
             exp_pair(i)
+            if i == LN_AT:
+                log_early()
+            if i == N_PAIRS - 2:
+                lse_early()
         finish_last()
-
-        lse = const.tile([P, N_TILES], F32, name="lse")
-        conf = const.tile([P, N_TILES], F32, name="conf")
-        nc.scalar.activation(out=lse[:], in_=zsum[:], func=ACT.Ln)
-        nc.vector.tensor_tensor(out=lse[:], in0=lse[:], in1=negm[:], op=ALU.subtract)
-        nc.scalar.activation(out=conf[:], in_=lse[:], func=ACT.Sigmoid, bias=t_b[:], scale=t_f[:])
         nc.sync.dma_start(
             out=out_1.rearrange("b (p r) -> p b r", p=P),
             in_=conf[:].rearrange("p (b r) -> p b r", b=B),

from contextlib import ExitStack

import concourse.mybir as mybir
from concourse.masks import make_identity

F32 = mybir.dt.float32
BF16 = mybir.dt.bfloat16
U32 = mybir.dt.uint32
U8 = mybir.dt.uint8
FP8X4 = mybir.dt.float8_e4m3fn_x4
ALU = mybir.AluOpType
ACT = mybir.ActivationFunctionType
AX = mybir.AxisListType

P = 128
B, Q, K, D = 2, 4096, 512, 1024
FLOPS = 2 * B * Q * K * D
R = 4
TILES_B = Q // P
CHUNKS_B = TILES_B // R
N_TILES = B * TILES_B
N_PAIRS = N_TILES // 2
BIG = 2.0 ** 120
LAG = 2
LN_AT = N_PAIRS - 4
N_EARLY = 2 * (LN_AT + 1)
N_LATE = N_TILES - N_EARLY
FIRST_TURNED = 9
TURNED_EVERY = 4
TURNED_BEFORE = LN_AT - 1
AHEAD = 8


def tile_contentattention_t_kernel(tc, queries, keys, temperature, bias, out_0, out_1):
    nc = tc.nc
    with ExitStack() as ctx:
        const = ctx.enter_context(tc.tile_pool(name="const", bufs=1))
        qpool = ctx.enter_context(tc.tile_pool(name="qpool", bufs=10))
        gpool = ctx.enter_context(tc.tile_pool(name="gpool", bufs=5))
        cpool = ctx.enter_context(tc.tile_pool(name="cpool", bufs=4))
        tpool = ctx.enter_context(tc.tile_pool(name="tpool", bufs=2))
        opool = ctx.enter_context(tc.tile_pool(name="opool", bufs=5))
        ps_t = ctx.enter_context(tc.psum_pool(name="ps_t", bufs=4))
        ps_l = ctx.enter_context(tc.psum_pool(name="ps_l", bufs=4))

        one = const.tile([P, 1], F32, name="one")
        junk = const.tile([P, 1], F32, name="junk")
        nc.vector.memset(one[:], 1.0)
        nc.scalar.activation(out=junk[:], in_=one[:], func=ACT.Exp)
        ident_f = const.tile([P, P], F32, name="ident_f")
        ident_b = const.tile([P, P], BF16, name="ident_b")
        make_identity(nc, ident_f[:])
        make_identity(nc, ident_b[:])

        k_sb = const.tile([P, B * 4 * D], BF16, name="k_sb")
        k32 = k_sb[:].bitcast(F32)
        zsum = const.tile([P, N_TILES], F32, name="zsum")
        negm = const.tile([P, N_TILES], F32, name="negm")
        rz = const.tile([P, N_TILES], F32, name="rz")
        t_bf = const.tile([P, 1], BF16, name="t_bf")
        b_bf = const.tile([P, 1], BF16, name="b_bf")
        t_n = const.tile([P, 1], F32, name="t_n")
        t_b = const.tile([P, 1], F32, name="t_b")
        lse = const.tile([P, N_EARLY], F32, name="lse")
        early = const.tile([P, N_EARLY], F32, name="early")
        late = const.tile([P, N_LATE], F32, name="late")
        conf = const.tile([P, N_TILES], F32, name="conf")
        den = const.tile([P, N_EARLY], F32, name="den")

        q_tiles = {}

        def load_keys(b, t, n):
            nc.sync.dma_start(
                out=k_sb[:, (b * 4 + t) * D : (b * 4 + t + n) * D].rearrange("p (t d) -> p t d", t=n),
                in_=keys[b][t * P : (t + n) * P, :].rearrange("(t p) d -> p t d", p=P),
            )

        def load_rows(c, r, n):
            b, cc = divmod(c, CHUNKS_B)
            if r == 0:
                q_sb = qpool.tile([P, R * D], BF16, name="q_sb")
                q_tiles[c] = q_sb
            nc.sync.dma_start(
                out=q_tiles[c][:, r * D : (r + n) * D],
                in_=queries[b].rearrange("(p r) d -> p (r d)", p=P)[:, (cc * R + r) * D : (cc * R + r + n) * D],
            )

        kcodes, kscl, caps, key_bias = {}, {}, {}, {}

        gks = {}

        def keys_cap(b):
            capv = const.tile([P, 4], BF16, name="capv%d" % b)
            first = k_sb[:, b * 4 * D : (b + 1) * 4 * D].rearrange("p (t d) -> p t d", t=4)[:, :, 0:1]
            nc.vector.tensor_scalar(out=capv[:].rearrange("p (t o) -> p t o", o=1), in0=first, scalar1=0.0, scalar2=-0.5, op0=ALU.not_equal, op1=ALU.add)
            bias_b = const.tile([P, 4], F32, name="key_bias%d" % b)
            nc.vector.tensor_scalar(out=bias_b[:].rearrange("p (t o) -> p t o", o=1), in0=first, scalar1=0.0, scalar2=-BIG, op0=ALU.is_equal, op1=ALU.mult)
            key_bias[b] = bias_b
            return capv

        def keys_cap_row(b, capv):
            cap_ps = ps_t.tile([P, K], F32, name="cap_ps", tag="xt")
            for t in range(4):
                nc.tensor.matmul(
                    out=cap_ps[:, t * P : (t + 1) * P],
                    lhsT=capv[:, t : t + 1].to_broadcast([P, P]),
                    rhs=ident_b[:],
                    start=True,
                    stop=True,
                )
            cap = const.tile([P, K], F32, name="cap%d" % b)
            nc.scalar.mul(out=cap[:], in_=cap_ps[:], mul=2.0 * BIG)
            caps[b] = cap

        def keys_transpose(b, t, on_vector):
            if t % 2 == 0:
                gk = const.tile([P, 2 * K * 2], BF16, name="gk%d_%d" % (b, t), align_bytes=64)
                gks[b, t // 2] = gk
            gk32 = gks[b, t // 2][:].bitcast(F32).rearrange("p (g j u) -> p g j u", g=2, u=2)
            xt = ps_t.tile([P, 2, 2, P], F32, name="xt", tag="xt")
            for w in range(4):
                col = (b * 4 + t) * (D // 2) + (w // 2) * 2 * P + w % 2
                nc.tensor.transpose(xt[:, w // 2, w % 2, :], k32[:, col : col + 2 * P - 1 : 2], ident_f[:])
            dst = gk32[:, :, (t % 2) * P : (t % 2 + 1) * P, :]
            src = xt[:].rearrange("p g u r -> p g r u")
            if on_vector:
                nc.vector.tensor_copy(out=dst, in_=src)
            else:
                nc.scalar.copy(out=dst, in_=src)

        def keys_quantise(b, h, g):
            if g == 0 and h == 0:
                kc = const.tile([P, 2 * K], U32, name="kc%d" % b, align_bytes=64)
                ks = const.tile([P, 2 * K], U8, name="ks%d" % b, align_bytes=64)
                kcodes[b], kscl[b] = kc, ks
            nc.vector.quantize_mx(
                out=kcodes[b][:, g * K + h * 2 * P : g * K + (h + 1) * 2 * P].bitcast(FP8X4),
                scales=kscl[b][:, g * K + h * 2 * P : g * K + (h + 1) * 2 * P],
                in_=gks[b, h][:, g * 8 * P : (g + 1) * 8 * P],
            )

        xts, grps, codes, scls, lgs, lts, outs = {}, {}, {}, {}, {}, {}, {}

        def turned(i):
            return FIRST_TURNED <= i < TURNED_BEFORE and (i - FIRST_TURNED) % TURNED_EVERY == 0

        def transpose_tile(t):
            i, tl = divmod(t, 2)
            if tl == 0:
                grp = gpool.tile([P, 2 * D], BF16, name="grp", align_bytes=64)
                grps[i] = grp
            q32 = q_tiles[t // R][:].bitcast(F32)
            xt = ps_t.tile([P, 2, 2, P], F32, name="xt", tag="xt")
            for w in range(4):
                col = (t % R) * (D // 2) + (w // 2) * 2 * P + w % 2
                nc.tensor.transpose(xt[:, w // 2, w % 2, :], q32[:, col : col + 2 * P - 1 : 2], ident_f[:])
            xts[t] = xt

        def copy_tile(t, on_vector):
            i, tl = divmod(t, 2)
            g32 = grps[i][:].bitcast(F32)
            if not turned(i):
                dst = g32[:, tl * 512 : (tl + 1) * 512].rearrange("p (g r u) -> p g r u", g=2, u=2)
            else:
                dst = g32.rearrange("p (g t r u) -> p g t r u", g=2, t=2, u=2)[:, :, tl, :, :]
            src = xts[t][:].rearrange("p g u r -> p g r u")
            if on_vector:
                nc.vector.tensor_copy(out=dst, in_=src)
            else:
                nc.scalar.copy(out=dst, in_=src)

        def transpose_pair(i):
            for t in (2 * i, 2 * i + 1):
                transpose_tile(t)

        def copy_pair(i):
            for t in (2 * i, 2 * i + 1):
                copy_tile(t, False)

        def quantise(i, tl, n):
            if tl == 0:
                cd = cpool.tile([P, 512], U32, name="cd", align_bytes=64)
                sc = cpool.tile([P, 512], U8, name="sc", align_bytes=64)
                codes[i], scls[i] = cd, sc
            nc.vector.quantize_mx(
                out=codes[i][:, tl * 256 : (tl + n) * 256].bitcast(FP8X4),
                scales=scls[i][:, tl * 256 : (tl + n) * 256],
                in_=grps[i][:, tl * D : (tl + n) * D],
            )

        def logits_turned(i):
            b = (2 * i) // TILES_B
            lt = tpool.tile([P, 4, 2 * P], F32, name="lt")
            for h in range(2):
                lg = ps_l.tile([P, K], F32, name="lg")
                for e in range(2):
                    kt = 2 * h + e
                    for g in range(2):
                        nc.tensor.matmul_mx(
                            out=lg[:, e * 2 * P : (e + 1) * 2 * P],
                            lhsT=kcodes[b][:, g * K + kt * P : g * K + (kt + 1) * P].bitcast(FP8X4),
                            lhsT_scale=kscl[b][:, g * K + kt * P : g * K + (kt + 1) * P],
                            rhs=codes[i][:, g * 2 * P : (g + 1) * 2 * P].bitcast(FP8X4),
                            rhs_scale=scls[i][:, g * 2 * P : (g + 1) * 2 * P],
                            start=(g == 0),
                            stop=(g == 1),
                        )
                for e in range(2):
                    kt = 2 * h + e
                    nc.scalar.activation(
                        out=lt[:, kt, :], in_=lg[:, e * 2 * P : (e + 1) * 2 * P], func=ACT.Identity,
                        bias=key_bias[b][:, kt : kt + 1], scale=1.0,
                    )
            lts[i] = lt

        def turn_back(i):
            for tl in range(2):
                lg = ps_l.tile([P, K], F32, name="lg")
                for kt in range(4):
                    nc.tensor.transpose(lg[:, kt * P : (kt + 1) * P], lts[i][:, kt, tl * P : (tl + 1) * P], ident_f[:])
                lgs[2 * i + tl] = lg

        def logits_pair(i):
            b = (2 * i) // TILES_B
            for tl in range(2):
                lg = ps_l.tile([P, K], F32, name="lg")
                for g in range(2):
                    s = (tl * 2 + g) * P
                    nc.tensor.matmul_mx(
                        out=lg[:],
                        lhsT=codes[i][:, s : s + P].bitcast(FP8X4),
                        lhsT_scale=scls[i][:, s : s + P],
                        rhs=kcodes[b][:, g * K : (g + 1) * K].bitcast(FP8X4),
                        rhs_scale=kscl[b][:, g * K : (g + 1) * K],
                        start=(g == 0),
                        stop=(g == 1),
                    )
                lgs[2 * i + tl] = lg

        def out_slice(t):
            return outs[t // R][:, (t % R) * K : (t % R + 1) * K]

        def mask_pair(i):
            b = (2 * i) // TILES_B
            if i % 2 == 0:
                ot = opool.tile([P, R * K], F32, name="ot")
                outs[i // 2] = ot
            for tl in range(2):
                t = 2 * i + tl
                if not turned(i):
                    nc.vector.tensor_tensor(out=out_slice(t), in0=lgs[t][:], in1=caps[b][:], op=ALU.min)

        def row_max(t):
            src = lgs[t][:] if turned(t // 2) else out_slice(t)
            nc.vector.tensor_reduce(out=negm[:, t : t + 1], in_=src, axis=AX.X, op=ALU.max, negate=True)

        def exp_pair(i):
            for tl in range(2):
                t = 2 * i + tl
                if t == N_TILES - 1:
                    exp_m_late()
                nc.scalar.activation(
                    out=out_slice(t), in_=lgs[t][:] if turned(i) else out_slice(t), func=ACT.Exp,
                    bias=negm[:, t : t + 1], scale=1.0, accum_out=zsum[:, t : t + 1],
                )

        def store(t0, n):
            b, r = divmod(t0, TILES_B)
            nc.sync.dma_start(
                out=out_0[b].rearrange("(p r) k -> p (r k)", p=P)[:, r * K : (r + n) * K],
                in_=outs[t0 // R][:, (t0 % R) * K : (t0 % R + n) * K],
            )

        def invert(t, n):
            nc.vector.reciprocal(out=rz[:, t : t + n], in_=zsum[:, t : t + n])

        def scale_tile(t, on_vector):
            o = out_slice(t)
            if on_vector:
                nc.vector.tensor_scalar_mul(out=o, in0=o, scalar1=rz[:, t : t + 1])
            else:
                nc.gpsimd.tensor_scalar(out=o, in0=o, scalar1=rz[:, t : t + 1], scalar2=0.0, op0=ALU.mult, op1=ALU.add)

        def store_pair(i):
            if i >= N_PAIRS - 4:
                store(2 * i, 2)
            elif i % 2 == 1:
                store(2 * i - 2, 4)

        def log_early():
            nc.scalar.activation(out=lse[:], in_=zsum[:, 0:N_EARLY], func=ACT.Ln)

        def lse_early():
            nc.gpsimd.tensor_tensor(out=lse[:], in0=lse[:], in1=negm[:, 0:N_EARLY], op=ALU.subtract)

        def conf_early():
            nc.scalar.activation(out=early[:], in_=lse[:], func=ACT.Exp, bias=t_b[:], scale=t_n[:])
            nc.gpsimd.tensor_scalar(out=den[:], in0=early[:], scalar1=1.0, scalar2=1.0, op0=ALU.mult, op1=ALU.add)

        def exp_m_late():
            nc.scalar.activation(out=late[:], in_=negm[:, N_EARLY:], func=ACT.Exp, bias=b_bf[:], scale=-1.0)

        last = const.tile([P, N_LATE], F32, name="last")
        last_p = const.tile([P, N_LATE], F32, name="last_p")

        def finish_last():
            t0 = N_TILES - 4
            invert(t0, 2)
            invert(t0 + 2, 1)
            for t in (t0, t0 + 1):
                scale_tile(t, True)
            store(t0, 2)
            nc.vector.tensor_tensor(out=last[:], in0=zsum[:, N_EARLY:], in1=late[:], op=ALU.mult)
            nc.gpsimd.tensor_tensor(out=last_p[:], in0=last[:], in1=t_n[:].to_broadcast([P, N_LATE]), op=ALU.pow)
            invert(t0 + 3, 1)
            for t in (t0 + 2, t0 + 3):
                nc.scalar.activation(out=out_slice(t), in_=out_slice(t), func=ACT.Copy, scale=rz[:, t : t + 1])
                store(t, 1)
            nc.vector.reciprocal(out=conf[:, 0:N_EARLY], in_=den[:])
            nc.vector.tensor_scalar_add(out=last[:], in0=last_p[:], scalar1=1.0)
            nc.vector.reciprocal(out=conf[:, N_EARLY:], in_=last[:])

        ctx.enter_context(tc.manual_schedule())
        load_rows(0, 0, 1)
        for t in range(4):
            load_keys(0, t, 1)
        load_rows(0, 1, 1)
        load_rows(0, 2, 1)
        load_rows(0, 3, 1)
        load_rows(1, 0, 2)
        load_rows(1, 2, 2)
        load_rows(2, 0, R)
        load_keys(1, 0, 4)
        nc.sync.dma_start(out=t_bf[:], in_=temperature.partition_broadcast(P))
        nc.sync.dma_start(out=b_bf[:], in_=bias.partition_broadcast(P))
        for c in range(3, AHEAD):
            load_rows(c, 0, R)

        transpose_tile(0)
        copy_tile(0, False)
        keys_transpose(0, 0, True)
        keys_transpose(0, 1, False)
        quantise(0, 0, 1)
        keys_transpose(0, 2, True)
        keys_transpose(0, 3, False)
        capv = keys_cap(0)
        for h in range(2):
            for g in range(2):
                keys_quantise(0, h, g)
        transpose_tile(1)
        copy_tile(1, False)
        quantise(0, 1, 1)
        keys_cap_row(0, capv)
        transpose_pair(1)
        copy_pair(1)
        logits_pair(0)
        transpose_pair(2)
        copy_pair(2)
        for i in range(N_PAIRS):
            if i % 2 == 0 and i // 2 + AHEAD < B * CHUNKS_B:
                load_rows(i // 2 + AHEAD, 0, R)
            if turned(i):
                turn_back(i)
            if i + 3 < N_PAIRS:
                transpose_pair(i + 3)
                if not turned(i + 1):
                    copy_pair(i + 3)
            if 4 <= i < 8:
                keys_transpose(1, i - 4, False)
            if i == 6:
                capv = keys_cap(1)
            if i == 8:
                keys_cap_row(1, capv)
            if 1 <= i < N_PAIRS - 1:
                quantise(i + 1, 0, 2)
            if 9 <= i < 11:
                for g in range(2):
                    keys_quantise(1, i - 9, g)
            if i == 12:
                nc.gpsimd.tensor_scalar(out=t_n[:], in0=t_bf[:], scalar1=-1.0, scalar2=0.0, op0=ALU.mult, op1=ALU.add)
                nc.gpsimd.tensor_tensor(out=t_b[:], in0=t_n[:], in1=b_bf[:], op=ALU.mult)
            if i >= LAG:
                j = i - LAG
                invert(2 * j, 2)
                scale_tile(2 * j, False)
                if not turned(i):
                    scale_tile(2 * j + 1, False)
                    store_pair(j)
            mask_pair(i)
            if i == 0:
                quantise(1, 0, 2)
            row_max(2 * i)
            if turned(i):
                scale_tile(2 * j + 1, True)
                store_pair(j)
            row_max(2 * i + 1)
            if i + 1 < N_PAIRS:
                if turned(i + 1):
                    logits_turned(i + 1)
                    if i + 3 < N_PAIRS:
                        copy_pair(i + 3)
                else:
                    logits_pair(i + 1)
            if i == N_PAIRS - 1:
                conf_early()
            exp_pair(i)
            if i == LN_AT:
                log_early()
            if i == N_PAIRS - 2:
                lse_early()
        finish_last()
        nc.sync.dma_start(
            out=out_1.rearrange("b (p r) -> p b r", p=P),
            in_=conf[:].rearrange("p (b r) -> p b r", b=B),
        )
